import numpy as np
import ml_dtypes


def mxq(x, axis, fmt="e4m3"):
    dtype, down = {"e4m3": (ml_dtypes.float8_e4m3fn, 7), "e5m2": (ml_dtypes.float8_e5m2, 14)}[fmt]
    v = np.moveaxis(np.asarray(x, np.float32).astype(ml_dtypes.bfloat16).astype(np.float64), axis, -1)
    blocks = v.reshape(v.shape[:-1] + (-1, 32))
    amax = np.abs(blocks).max(-1, keepdims=True)
    byte = np.maximum(np.where(amax > 0, np.frexp(amax)[1] - 1 + 127, 0) - down, 1)
    scale = np.exp2(byte - 127.0)
    codes = (blocks / scale).astype(np.float32).astype(dtype).astype(np.float64)
    return np.moveaxis((codes * scale).reshape(v.shape), -1, axis)


WIDE = False


def mx_kscale(k):
    if not WIDE:
        return np.ones(k)
    levels = np.array([10, -10, 5, -5, 0])
    a = np.random.permutation(np.resize(levels, k // 512 * 4)).reshape(k // 512, 4)
    idx = np.arange(k)
    return np.exp2(a[idx // 512, idx % 128 // 32])


BF16 = ml_dtypes.bfloat16


def bf(x):
    return np.asarray(x, np.float32).astype(BF16)


def f64(x):
    return np.asarray(x).astype(np.float64)


N, LMAX, CIN, COUT = 512, 3, 1024, 128
NL = LMAX + 1
NM = NL * NL


def setup_inputs():
    s = mx_kscale(CIN)
    return {"x": bf(np.random.standard_normal((N, NM, CIN)) * s),
            "weights": bf(np.random.standard_normal((NL, CIN, COUT)) / np.sqrt(CIN) / s[:, None]),
            "path_weights": bf(1.0 + 0.3 * np.random.standard_normal(NL))}


def reference(x, weights, path_weights):
    x, weights, path_weights = f64(x), f64(weights), f64(path_weights)
    blocks = []
    for l in range(LMAX + 1):
        start = l * l
        end = start + (2 * l + 1)
        blk = mxq(x[:, start:end, :], 2, "e4m3") @ mxq(weights[l], 0, "e4m3")
        blocks.append(path_weights[l] * blk)
    return np.concatenate(blocks, axis=1)

@@ -1,0 +1,155 @@
+import concourse.mybir as mybir
+from concourse.masks import make_identity
+
+BF16 = mybir.dt.bfloat16
+F32 = mybir.dt.float32
+U32 = mybir.dt.uint32
+U8 = mybir.dt.uint8
+FP8X4 = mybir.dt.float8_e4m3fn_x4
+
+NODES, ROWS, CIN, COUT, DEGREES = 512, 16, 1024, 128, 4
+FLOPS = 2 * NODES * ROWS * CIN * COUT
+
+P = 128
+PACK = 4
+K_PASS = P * PACK
+PASSES = CIN // K_PASS
+WORDS = CIN // 2
+HALVES = PACK // 2
+
+DEGREE_OF_ROW = [l for l in range(DEGREES) for i in range(2 * l + 1)]
+
+UNITS = 4
+ROUNDS_PER_NODE_TILE = ROWS // UNITS
+ROUNDS = (NODES // P) * ROUNDS_PER_NODE_TILE
+
+
+def tile_linear_pa_t_kernel(tc, x, weights, path_weights, out):
+    nc = tc.nc
+    with (
+        tc.tile_pool(name="const", bufs=1) as const,
+        tc.tile_pool(name="x_pool", bufs=ROUNDS) as x_pool,
+        tc.tile_pool(name="grouped_pool", bufs=3) as grouped_pool,
+        tc.tile_pool(name="quantised_pool", bufs=3) as quantised_pool,
+        tc.tile_pool(name="out_pool", bufs=NODES // P) as out_pool,
+        tc.psum_pool(name="xt_pool", bufs=6) as xt_pool,
+        tc.psum_pool(name="acc_pool", bufs=2) as acc_pool,
+    ):
+        w_raw = const.tile([P, DEGREES * CIN], BF16)
+        nc.sync.dma_start(
+            out=w_raw[:].rearrange("p (a ec) -> p a ec", ec=2 * COUT),
+            in_=weights.rearrange("l k c -> (l k) c").rearrange("(a p e) c -> p a (e c)", p=P, e=2),
+        )
+        pw_bf16 = const.tile([P, DEGREES], BF16)
+        nc.scalar.dma_start(out=pw_bf16[:], in_=path_weights.partition_broadcast(P))
+
+        x_tiles = []
+        for r in range(ROUNDS):
+            n0 = (r // ROUNDS_PER_NODE_TILE) * P
+            m0 = (r % ROUNDS_PER_NODE_TILE) * UNITS
+            x_sb = x_pool.tile([P, UNITS * CIN], BF16)
+            nc.sync.dma_start(
+                out=x_sb[:], in_=x[n0 : n0 + P, m0 : m0 + UNITS, :].rearrange("n m k -> n (m k)")
+            )
+            x_tiles.append(x_sb)
+
+        ident = const.tile([P, P], F32)
+        make_identity(nc, ident[:])
+        pw = const.tile([P, DEGREES], F32)
+        nc.vector.tensor_copy(out=pw[:], in_=pw_bf16[:])
+
+        w_grouped = const.tile([P, DEGREES * CIN], BF16, align_bytes=64)
+        nc.vector.tensor_copy(
+            out=w_grouped[:].rearrange("p (b c t) -> p b c t", c=COUT, t=PACK),
+            in_=w_raw[:].rearrange("p (b t c) -> p b c t", c=COUT, t=PACK),
+        )
+        w_codes = const.tile([P, DEGREES * PASSES * COUT], U32, align_bytes=64)
+        w_scales = const.tile([P, DEGREES * PASSES * COUT], U8, align_bytes=64)
+        nc.vector.quantize_mx(out=w_codes[:].bitcast(FP8X4), scales=w_scales[:], in_=w_grouped[:])
+
+        def transpose_round(r):
+            x_words = x_tiles[r][:].bitcast(F32)
+            grouped = grouped_pool.tile([P, UNITS * CIN], BF16, align_bytes=64)
+            for unit in range(UNITS):
+                xt = xt_pool.tile([P, WORDS], F32)
+                for j in range(WORDS // P):
+                    nc.tensor.transpose(
+                        xt[:, j * P : (j + 1) * P],
+                        x_words[:, unit * WORDS + j * P : unit * WORDS + (j + 1) * P],
+                        ident[:],
+                    )
+                copy = nc.vector.tensor_copy if unit == 0 else nc.scalar.copy
+                copy(
+                    out=grouped[:, unit * CIN : (unit + 1) * CIN]
+                    .bitcast(F32)
+                    .rearrange("p (g n u) -> p g n u", g=PASSES, u=HALVES),
+                    in_=xt[:].rearrange("p (g u n) -> p g n u", g=PASSES, u=HALVES),
+                )
+            return grouped
+
+        def quantise_round(grouped):
+            codes = quantised_pool.tile([P, UNITS * PASSES * P], U32, align_bytes=64)
+            scales = quantised_pool.tile([P, UNITS * PASSES * P], U8, align_bytes=64)
+            nc.vector.quantize_mx(out=codes[:].bitcast(FP8X4), scales=scales[:], in_=grouped[:])
+            return codes, scales
+
+        def multiply_round(r, codes, scales, out_sb):
+            m0 = (r % ROUNDS_PER_NODE_TILE) * UNITS
+            acc = acc_pool.tile([P, UNITS * COUT], F32)
+            for unit in range(UNITS):
+                l = DEGREE_OF_ROW[m0 + unit]
+                for g in range(PASSES):
+                    x_cols = slice((unit * PASSES + g) * P, (unit * PASSES + g + 1) * P)
+                    w_cols = slice((l * PASSES + g) * COUT, (l * PASSES + g + 1) * COUT)
+                    nc.tensor.matmul_mx(
+                        out=acc[:, unit * COUT : (unit + 1) * COUT],
+                        lhsT=codes[:, x_cols].bitcast(FP8X4),
+                        lhsT_scale=scales[:, x_cols],
+                        rhs=w_codes[:, w_cols].bitcast(FP8X4),
+                        rhs_scale=w_scales[:, w_cols],
+                        start=(g == 0),
+                        stop=(g == PASSES - 1),
+                    )
+            for l in range(DEGREES):
+                units_of_l = [unit for unit in range(UNITS) if DEGREE_OF_ROW[m0 + unit] == l]
+                if not units_of_l:
+                    continue
+                first, count = units_of_l[0], len(units_of_l)
+                src = acc[:, first * COUT : (first + count) * COUT]
+                dst = out_sb[:, (m0 + first) * COUT : (m0 + first + count) * COUT]
+                if r % 2 == 0:
+                    nc.vector.tensor_scalar(
+                        out=dst, in0=src, scalar1=pw[:, l : l + 1], scalar2=None, op0=mybir.AluOpType.mult
+                    )
+                else:
+                    nc.scalar.activation(
+                        out=dst, in_=src, func=mybir.ActivationFunctionType.Copy, scale=pw[:, l : l + 1]
+                    )
+
+        def store_rows(r, out_sb, first_row, rows):
+            n0 = (r // ROUNDS_PER_NODE_TILE) * P
+            nc.sync.dma_start(
+                out=out[n0 : n0 + P, first_row : first_row + rows, :].rearrange("n m c -> n (m c)"),
+                in_=out_sb[:, first_row * COUT : (first_row + rows) * COUT],
+            )
+
+        grouped_of = {}
+        quantised_of = {}
+        out_of = {}
+        for s in range(ROUNDS + 2):
+            if s < ROUNDS:
+                grouped_of[s] = transpose_round(s)
+            if 1 <= s <= ROUNDS:
+                quantised_of[s - 1] = quantise_round(grouped_of[s - 1])
+            if s >= 2:
+                r = s - 2
+                node_tile = r // ROUNDS_PER_NODE_TILE
+                if r % ROUNDS_PER_NODE_TILE == 0:
+                    out_sb = out_pool.tile([P, ROWS * COUT], F32)
+                    out_of[node_tile] = out_sb
+                codes, scales = quantised_of[r]
+                multiply_round(r, codes, scales, out_of[node_tile])
+                if node_tile == NODES // P - 1:
+                    store_rows(r, out_of[node_tile], (r % ROUNDS_PER_NODE_TILE) * UNITS, UNITS)
+                elif r % ROUNDS_PER_NODE_TILE == ROUNDS_PER_NODE_TILE - 1:
+                    store_rows(r, out_of[node_tile], 0, ROWS)

@@ -34,6 +34,7 @@ def tile_linear_pa_t_kernel(tc, x, weights, path_weights, out):
         tc.tile_pool(name="out_pool", bufs=NODES // P) as out_pool,
         tc.psum_pool(name="xt_pool", bufs=6) as xt_pool,
         tc.psum_pool(name="acc_pool", bufs=2) as acc_pool,
+        tc.manual_schedule(),
     ):
         w_raw = const.tile([P, DEGREES * CIN], BF16)
         nc.sync.dma_start(

@@ -36,23 +36,28 @@ def tile_linear_pa_t_kernel(tc, x, weights, path_weights, out):
         tc.psum_pool(name="acc_pool", bufs=2) as acc_pool,
         tc.manual_schedule(),
     ):
-        w_raw = const.tile([P, DEGREES * CIN], BF16)
-        nc.sync.dma_start(
-            out=w_raw[:].rearrange("p (a ec) -> p a ec", ec=2 * COUT),
-            in_=weights.rearrange("l k c -> (l k) c").rearrange("(a p e) c -> p a (e c)", p=P, e=2),
-        )
-        pw_bf16 = const.tile([P, DEGREES], BF16)
-        nc.scalar.dma_start(out=pw_bf16[:], in_=path_weights.partition_broadcast(P))
-
-        x_tiles = []
-        for r in range(ROUNDS):
+        def load_x_round(r):
             n0 = (r // ROUNDS_PER_NODE_TILE) * P
             m0 = (r % ROUNDS_PER_NODE_TILE) * UNITS
             x_sb = x_pool.tile([P, UNITS * CIN], BF16)
             nc.sync.dma_start(
                 out=x_sb[:], in_=x[n0 : n0 + P, m0 : m0 + UNITS, :].rearrange("n m k -> n (m k)")
             )
-            x_tiles.append(x_sb)
+            return x_sb
+
+        x_tiles = [load_x_round(0)]
+
+        w_raw = const.tile([P, DEGREES * CIN], BF16)
+        for l in range(DEGREES):
+            nc.sync.dma_start(
+                out=w_raw[:, l * CIN : (l + 1) * CIN].rearrange("p (a ec) -> p a ec", ec=2 * COUT),
+                in_=weights[l].rearrange("(a p e) c -> p a (e c)", p=P, e=2),
+            )
+        pw_bf16 = const.tile([P, DEGREES], BF16)
+        nc.scalar.dma_start(out=pw_bf16[:], in_=path_weights.partition_broadcast(P))
+
+        for r in range(1, ROUNDS):
+            x_tiles.append(load_x_round(r))
 
         ident = const.tile([P, P], F32)
         make_identity(nc, ident[:])
@@ -60,10 +65,11 @@ def tile_linear_pa_t_kernel(tc, x, weights, path_weights, out):
         nc.vector.tensor_copy(out=pw[:], in_=pw_bf16[:])
 
         w_grouped = const.tile([P, DEGREES * CIN], BF16, align_bytes=64)
-        nc.vector.tensor_copy(
-            out=w_grouped[:].rearrange("p (b c t) -> p b c t", c=COUT, t=PACK),
-            in_=w_raw[:].rearrange("p (b t c) -> p b c t", c=COUT, t=PACK),
-        )
+        for l in range(DEGREES):
+            nc.vector.tensor_copy(
+                out=w_grouped[:, l * CIN : (l + 1) * CIN].rearrange("p (g c t) -> p g c t", c=COUT, t=PACK),
+                in_=w_raw[:, l * CIN : (l + 1) * CIN].rearrange("p (g t c) -> p g c t", c=COUT, t=PACK),
+            )
         w_codes = const.tile([P, DEGREES * PASSES * COUT], U32, align_bytes=64)
         w_scales = const.tile([P, DEGREES * PASSES * COUT], U8, align_bytes=64)
         nc.vector.quantize_mx(out=w_codes[:].bitcast(FP8X4), scales=w_scales[:], in_=w_grouped[:])

import concourse.mybir as mybir
from concourse.masks import make_identity

BF16 = mybir.dt.bfloat16
F32 = mybir.dt.float32
U32 = mybir.dt.uint32
U8 = mybir.dt.uint8
FP8X4 = mybir.dt.float8_e4m3fn_x4

NODES, ROWS, CIN, COUT, DEGREES = 512, 16, 1024, 128, 4
FLOPS = 2 * NODES * ROWS * CIN * COUT

P = 128
PACK = 4
K_PASS = P * PACK
PASSES = CIN // K_PASS
WORDS = CIN // 2
HALVES = PACK // 2

DEGREE_OF_ROW = [l for l in range(DEGREES) for i in range(2 * l + 1)]

UNITS = 4
ROUNDS_PER_NODE_TILE = ROWS // UNITS
ROUNDS = (NODES // P) * ROUNDS_PER_NODE_TILE


def tile_linear_pa_t_kernel(tc, x, weights, path_weights, out):
    nc = tc.nc
    with (
        tc.tile_pool(name="const", bufs=1) as const,
        tc.tile_pool(name="x_pool", bufs=ROUNDS) as x_pool,
        tc.tile_pool(name="grouped_pool", bufs=3) as grouped_pool,
        tc.tile_pool(name="quantised_pool", bufs=3) as quantised_pool,
        tc.tile_pool(name="out_pool", bufs=NODES // P) as out_pool,
        tc.psum_pool(name="xt_pool", bufs=6) as xt_pool,
        tc.psum_pool(name="acc_pool", bufs=2) as acc_pool,
        tc.manual_schedule(),
    ):
        def load_x_round(r):
            n0 = (r // ROUNDS_PER_NODE_TILE) * P
            m0 = (r % ROUNDS_PER_NODE_TILE) * UNITS
            x_sb = x_pool.tile([P, UNITS * CIN], BF16)
            nc.sync.dma_start(
                out=x_sb[:], in_=x[n0 : n0 + P, m0 : m0 + UNITS, :].rearrange("n m k -> n (m k)")
            )
            return x_sb

        x_tiles = [load_x_round(0)]

        w_raw = const.tile([P, DEGREES * CIN], BF16)
        for l in range(DEGREES):
            nc.sync.dma_start(
                out=w_raw[:, l * CIN : (l + 1) * CIN].rearrange("p (a ec) -> p a ec", ec=2 * COUT),
                in_=weights[l].rearrange("(a p e) c -> p a (e c)", p=P, e=2),
            )
        pw_bf16 = const.tile([P, DEGREES], BF16)
        nc.scalar.dma_start(out=pw_bf16[:], in_=path_weights.partition_broadcast(P))

        for r in range(1, ROUNDS):
            x_tiles.append(load_x_round(r))

        ident = const.tile([P, P], F32)
        make_identity(nc, ident[:])
        pw = const.tile([P, DEGREES], F32)
        nc.vector.tensor_copy(out=pw[:], in_=pw_bf16[:])

        w_grouped = const.tile([P, DEGREES * CIN], BF16, align_bytes=64)
        for l in range(DEGREES):
            nc.vector.tensor_copy(
                out=w_grouped[:, l * CIN : (l + 1) * CIN].rearrange("p (g c t) -> p g c t", c=COUT, t=PACK),
                in_=w_raw[:, l * CIN : (l + 1) * CIN].rearrange("p (g t c) -> p g c t", c=COUT, t=PACK),
            )
        w_codes = const.tile([P, DEGREES * PASSES * COUT], U32, align_bytes=64)
        w_scales = const.tile([P, DEGREES * PASSES * COUT], U8, align_bytes=64)
        nc.vector.quantize_mx(out=w_codes[:].bitcast(FP8X4), scales=w_scales[:], in_=w_grouped[:])

        def transpose_round(r):
            x_words = x_tiles[r][:].bitcast(F32)
            grouped = grouped_pool.tile([P, UNITS * CIN], BF16, align_bytes=64)
            for unit in range(UNITS):
                xt = xt_pool.tile([P, WORDS], F32)
                for j in range(WORDS // P):
                    nc.tensor.transpose(
                        xt[:, j * P : (j + 1) * P],
                        x_words[:, unit * WORDS + j * P : unit * WORDS + (j + 1) * P],
                        ident[:],
                    )
                copy = nc.vector.tensor_copy if unit == 0 else nc.scalar.copy
                copy(
                    out=grouped[:, unit * CIN : (unit + 1) * CIN]
                    .bitcast(F32)
                    .rearrange("p (g n u) -> p g n u", g=PASSES, u=HALVES),
                    in_=xt[:].rearrange("p (g u n) -> p g n u", g=PASSES, u=HALVES),
                )
            return grouped

        def quantise_round(grouped):
            codes = quantised_pool.tile([P, UNITS * PASSES * P], U32, align_bytes=64)
            scales = quantised_pool.tile([P, UNITS * PASSES * P], U8, align_bytes=64)
            nc.vector.quantize_mx(out=codes[:].bitcast(FP8X4), scales=scales[:], in_=grouped[:])
            return codes, scales

        def multiply_round(r, codes, scales, out_sb):
            m0 = (r % ROUNDS_PER_NODE_TILE) * UNITS
            acc = acc_pool.tile([P, UNITS * COUT], F32)
            for unit in range(UNITS):
                l = DEGREE_OF_ROW[m0 + unit]
                for g in range(PASSES):
                    x_cols = slice((unit * PASSES + g) * P, (unit * PASSES + g + 1) * P)
                    w_cols = slice((l * PASSES + g) * COUT, (l * PASSES + g + 1) * COUT)
                    nc.tensor.matmul_mx(
                        out=acc[:, unit * COUT : (unit + 1) * COUT],
                        lhsT=codes[:, x_cols].bitcast(FP8X4),
                        lhsT_scale=scales[:, x_cols],
                        rhs=w_codes[:, w_cols].bitcast(FP8X4),
                        rhs_scale=w_scales[:, w_cols],
                        start=(g == 0),
                        stop=(g == PASSES - 1),
                    )
            for l in range(DEGREES):
                units_of_l = [unit for unit in range(UNITS) if DEGREE_OF_ROW[m0 + unit] == l]
                if not units_of_l:
                    continue
                first, count = units_of_l[0], len(units_of_l)
                src = acc[:, first * COUT : (first + count) * COUT]
                dst = out_sb[:, (m0 + first) * COUT : (m0 + first + count) * COUT]
                if r % 2 == 0:
                    nc.vector.tensor_scalar(
                        out=dst, in0=src, scalar1=pw[:, l : l + 1], scalar2=None, op0=mybir.AluOpType.mult
                    )
                else:
                    nc.scalar.activation(
                        out=dst, in_=src, func=mybir.ActivationFunctionType.Copy, scale=pw[:, l : l + 1]
                    )

        def store_rows(r, out_sb, first_row, rows):
            n0 = (r // ROUNDS_PER_NODE_TILE) * P
            nc.sync.dma_start(
                out=out[n0 : n0 + P, first_row : first_row + rows, :].rearrange("n m c -> n (m c)"),
                in_=out_sb[:, first_row * COUT : (first_row + rows) * COUT],
            )

        grouped_of = {}
        quantised_of = {}
        out_of = {}
        for s in range(ROUNDS + 2):
            if s < ROUNDS:
                grouped_of[s] = transpose_round(s)
            if 1 <= s <= ROUNDS:
                quantised_of[s - 1] = quantise_round(grouped_of[s - 1])
            if s >= 2:
                r = s - 2
                node_tile = r // ROUNDS_PER_NODE_TILE
                if r % ROUNDS_PER_NODE_TILE == 0:
                    out_sb = out_pool.tile([P, ROWS * COUT], F32)
                    out_of[node_tile] = out_sb
                codes, scales = quantised_of[r]
                multiply_round(r, codes, scales, out_of[node_tile])
                if node_tile == NODES // P - 1:
                    store_rows(r, out_of[node_tile], (r % ROUNDS_PER_NODE_TILE) * UNITS, UNITS)
                elif r % ROUNDS_PER_NODE_TILE == ROUNDS_PER_NODE_TILE - 1:
                    store_rows(r, out_of[node_tile], 0, ROWS)
